import numpy as np
import ml_dtypes


def mxq(x, axis, fmt="e4m3"):
    dtype, down = {"e4m3": (ml_dtypes.float8_e4m3fn, 7), "e5m2": (ml_dtypes.float8_e5m2, 14)}[fmt]
    v = np.moveaxis(np.asarray(x, np.float32).astype(ml_dtypes.bfloat16).astype(np.float64), axis, -1)
    blocks = v.reshape(v.shape[:-1] + (-1, 32))
    amax = np.abs(blocks).max(-1, keepdims=True)
    byte = np.maximum(np.where(amax > 0, np.frexp(amax)[1] - 1 + 127, 0) - down, 1)
    scale = np.exp2(byte - 127.0)
    codes = (blocks / scale).astype(np.float32).astype(dtype).astype(np.float64)
    return np.moveaxis((codes * scale).reshape(v.shape), -1, axis)


WIDE = False


def mx_kscale(k):
    if not WIDE:
        return np.ones(k)
    levels = np.array([18, -18])
    if k % 512:
        return np.exp2(np.random.permutation(np.resize(levels, k // 32))).repeat(32)
    a = np.empty((k // 512, 16))
    for p in range(k // 512):
        a[p, :8] = np.random.permutation(np.resize(levels, 8))
        for g in range(8):
            far = levels[np.abs(levels - a[p, g]) >= 10]
            a[p, g + 8] = far[np.random.randint(len(far))]
    return np.exp2(a.ravel()).repeat(32)


BF16 = ml_dtypes.bfloat16


def bf(x):
    return np.asarray(x, np.float32).astype(BF16)


def f64(x):
    return np.asarray(x).astype(np.float64)


T, N, D, E, OUT = 4, 512, 512, 2, 256
H0 = 2 * OUT
C = (E + 1) * D
EPS = 1e-12
SLOPE = 0.01


def leaky_relu(v):
    return np.where(v >= 0.0, v, SLOPE * v)


def setup_inputs():
    u = mx_kscale(H0)
    v = mx_kscale(D)
    s = mx_kscale(T * N).reshape(T, N)
    cls = np.where(np.random.random((T, N)) < 0.5, -1.0, 1.0)
    pat = np.where(np.random.random((T, 1, D)) < 0.5, -1.0, 1.0)
    nf0 = bf(1.0 + 0.6 * cls[:, :, None] * pat + 0.4 * np.random.standard_normal((T, N, D)))
    same = cls[:, None, :, None] * cls[:, None, None, :]
    chan = ((-1.0) ** np.arange(E))[None, :, None, None]
    edge = (0.5 + 0.5 * np.random.random((T, E, N, N))) * (1.0 + 0.6 * chan * same)
    edge = edge * np.where(np.random.random((T, E, N, N)) < 0.05, -1.0, 1.0)
    e0 = bf(edge + 0.1 * N * np.eye(N))
    w_scale = np.where(np.arange(C) < D, 1.0, 16.0)
    w0_0 = bf(np.random.standard_normal((H0, C)) / np.sqrt(C) * w_scale)
    g = bf(4.0 * np.random.standard_normal((T, N, H0)) * np.exp2(np.random.randint(-6, 1, (T, N, 1))) / s[:, :, None] * u)
    masked = f64(e0) * (1.0 - np.eye(N))
    denom = np.maximum(np.abs(masked).sum(-1), EPS)
    aggr = (masked @ f64(nf0)[:, None]) / denom[..., None]
    x = np.concatenate([f64(nf0), aggr.transpose(0, 2, 1, 3).reshape(T, N, E * D)], axis=-1)
    z = x @ f64(w0_0).T
    cols = np.tile(v, E + 1)
    cols[:D] = cols[:D] * np.min(s)
    return {"node_feat": bf(f64(nf0) / v), "edge_feat": bf(f64(e0) * s[:, None, :, None]), "w0": bf(f64(w0_0) * cols / u[:, None]),
            "denom": np.asarray(denom, np.float32), "z": np.asarray(z, np.float32), "grad_out": g}


def reference(node_feat, edge_feat, w0, denom, z, grad_out):
    off = 1.0 - np.eye(N)
    masked = f64(edge_feat) * off
    den = f64(denom)[..., None]
    dz2 = f64(grad_out) * np.where(f64(z) >= 0.0, 1.0, SLOPE)
    dx = mxq(dz2, 2, "e5m2") @ mxq(f64(w0), 0, "e4m3")
    daggr = dx[:, :, D:].reshape(T, N, E, D).transpose(0, 2, 1, 3)
    dz1 = (daggr / den).reshape(T, E * N, D)
    agg_road = mxq(masked.reshape(T, E * N, N), 1, "e4m3").transpose(0, 2, 1) @ mxq(dz1, 1, "e5m2")
    dnode = dx[:, :, :D] + agg_road
    dm = (mxq(dz1, 2, "e5m2") @ mxq(f64(node_feat), 2, "e4m3").transpose(0, 2, 1)).reshape(T, E, N, N)
    r = (dm * masked).sum(-1, keepdims=True) / den
    dedge = (dm - np.sign(masked) * r) * off
    return dnode, dedge

@@ -1,0 +1,424 @@
+from contextlib import ExitStack
+
+import concourse.mybir as mybir
+from concourse.masks import make_identity
+
+T, N, D, E, H = 4, 512, 512, 2, 512
+C = (E + 1) * D
+SLOPE = 0.01
+FLOPS = 2 * T * N * H * C + 2 * 2 * T * E * N * N * D
+
+F32 = mybir.dt.float32
+BF16 = mybir.dt.bfloat16
+U32 = mybir.dt.uint32
+U8 = mybir.dt.uint8
+E4 = mybir.dt.float8_e4m3fn_x4
+E5 = mybir.dt.float8_e5m2_x4
+ALU = mybir.AluOpType
+ACT = mybir.ActivationFunctionType
+
+P = 128
+J = 4
+W = 512
+SKEW = W + J
+PADDED = J * SKEW
+
+
+def tile_nodeupdatenetwork_pa_v_kernel(tc, node_feat, edge_feat, w0, denom, z, grad_out, out_0, out_1):
+    nc = tc.nc
+
+    with ExitStack() as ctx:
+        const = ctx.enter_context(tc.tile_pool(name="const", bufs=1))
+        load = ctx.enter_context(tc.tile_pool(name="load", bufs=2))
+        work = ctx.enter_context(tc.tile_pool(name="work", bufs=2))
+        quant = ctx.enter_context(tc.tile_pool(name="quant", bufs=2))
+        psum = ctx.enter_context(tc.psum_pool(name="psum", bufs=1))
+
+        def node_rows(rows, i):
+            return rows.rearrange("(k j i) w -> i k j w", j=J, i=J)[i]
+
+        def slots(buf):
+            return buf[:, 0 : J * W].rearrange("p (j w) -> p j w", j=J)
+
+        def load_nodes(buf, rows):
+            for i in range(J):
+                nc.sync.dma_start(out=slots(buf)[i:P:J], in_=node_rows(rows, i))
+
+        def store_nodes(rows, buf, js):
+            for i in range(J):
+                nc.sync.dma_start(out=node_rows(rows, i)[:, js], in_=slots(buf)[i:P:J, js])
+
+        def diagonal_runs(buf):
+            return buf[:].rearrange("p (j x) -> p j x", x=SKEW)[:, :, 0:W].rearrange("p j (k y) -> p j k y", y=16)[:, :, :, 0:J]
+
+        def quantize(grouped, fmt, tag, bufs):
+            codes = quant.tile([P, W], U32, name=tag + "_codes", tag=tag + "_codes", bufs=bufs, align_bytes=64)
+            scales = quant.tile([P, W], U8, name=tag + "_scales", tag=tag + "_scales", bufs=bufs, align_bytes=64)
+            nc.vector.quantize_mx(out=codes[:].bitcast(fmt), scales=scales[:], in_=grouped[:])
+            return codes, scales, fmt
+
+        def mx_pass(acc, stationary, j, moving, start, stop):
+            cols = slice(j * P, (j + 1) * P)
+            nc.tensor.matmul_mx(
+                out=acc[:],
+                lhsT=stationary[0][:, cols].bitcast(stationary[2]),
+                lhsT_scale=stationary[1][:, cols],
+                rhs=moving[0][:].bitcast(moving[2]),
+                rhs_scale=moving[1][:],
+                start=start,
+                stop=stop,
+            )
+
+        def grouped_tile():
+            return work.tile([P, J * W], BF16, name="grouped", tag="grouped", bufs=7, align_bytes=64)
+
+        def copy_on(engine, out, in_):
+            if engine == "vector":
+                nc.vector.tensor_copy(out=out, in_=in_)
+            else:
+                nc.scalar.copy(out=out, in_=in_)
+
+        def turn_half(rows, word_block, grouped, half):
+            words = rows[:, 0 : J * W].bitcast(F32).rearrange("p (j w) -> p j w", j=J)
+            dst = grouped[:].bitcast(F32).rearrange("q (j p u) -> q j p u", j=J, u=2)
+            bank = psum.tile([P, 2, 2, P], F32, name="turn_bank", tag="bank", bufs=4)
+            for jj in range(2):
+                for u in range(2):
+                    nc.tensor.transpose(bank[:, jj, u, :], word_block(words[:, 2 * half + jj, :], u), ident[:])
+            nc.scalar.copy(out=dst[:, 2 * half : 2 * half + 2], in_=bank[:].rearrange("q j u p -> q j p u"))
+
+        def turn(rows, word_block):
+            grouped = grouped_tile()
+            for half in range(2):
+                turn_half(rows, word_block, grouped, half)
+            return grouped
+
+        def every_second(words, u):
+            return words[:, u : W // 2 : 2]
+
+        def contiguous(words, u):
+            return words[:, u * P : (u + 1) * P]
+
+        def interleave(engine, src, dst):
+            if engine == "gpsimd":
+                for a in range(4):
+                    n = src.shape[1] // 4
+                    s1 = src[:, a] if n == 1 else src[:, a * n : (a + 1) * n]
+                    d1 = dst[:, a] if n == 1 else dst[:, a * n : (a + 1) * n]
+                    nc.gpsimd.tensor_scalar(out=d1, in0=s1, scalar1=1.0, scalar2=0.0, op0=ALU.mult, op1=ALU.add)
+            elif engine == "both":
+                n = src.shape[1] // 2
+                nc.scalar.copy(out=dst[:, 0:n], in_=src[:, 0:n])
+                nc.vector.tensor_copy(out=dst[:, n : 2 * n], in_=src[:, n : 2 * n])
+            else:
+                copy_on(engine, dst, src)
+
+        g_t, z_t, nf_t, edge_t, w_raw = {}, {}, {}, {}, {}
+
+        def load_gz(t):
+            z_t[t] = load.tile([P, J * W], F32, name="z_rows", tag="z_rows")
+            load_nodes(z_t[t], z[t])
+            g_t[t] = load.tile([P, J * W], BF16, name="g_rows", tag="g_rows")
+            load_nodes(g_t[t], grad_out[t])
+
+        def load_nf(t):
+            nf_t[t] = load.tile([P, J * W], BF16, name="nf_rows", tag="nf_rows")
+            nc.sync.dma_start(out=slots(nf_t[t]), in_=node_feat[t].rearrange("(k p) d -> p k d", p=P))
+
+        def load_edge(s):
+            edge_t[s] = load.tile([P, J * W], BF16, name="edge_rows", tag="edge_rows", bufs=5)
+            load_nodes(edge_t[s], edge_feat[s // E, s % E])
+
+        def load_w(c):
+            w_raw[c] = load.tile([P, J * W], BF16, name="w_rows", tag="w_rows", bufs=3)
+            nc.sync.dma_start(out=slots(w_raw[c]), in_=w0[:, c * W : (c + 1) * W].rearrange("(p j) c -> p j c", j=J))
+
+        ctx.enter_context(tc.manual_schedule())
+
+        den_rows = const.tile([T * E, N], F32, name="den_rows")
+        load_w(1)
+        nc.sync.dma_start(out=den_rows[:], in_=denom.rearrange("t e n -> (t e) n"))
+        load_edge(0)
+        load_gz(0)
+        load_nf(0)
+        load_w(2)
+        load_edge(1)
+        load_w(0)
+        load_gz(1)
+        load_nf(1)
+        load_edge(2)
+        load_edge(3)
+        ident = const.tile([P, P], F32, name="ident")
+        make_identity(nc, ident[:])
+        den_sorted = const.tile([P, N], F32, name="den_sorted")
+        nc.gpsimd.memset(den_sorted[:], 1.0)
+        off = const.tile([P, J, P], BF16, name="off")
+        for j in range(J):
+            nc.vector.tensor_scalar(out=off[:, j, :], in0=ident[:], scalar1=-1.0, scalar2=1.0, op0=ALU.mult, op1=ALU.add)
+        ident_bf = const.tile([P, P], BF16, name="ident_bf")
+        nc.vector.tensor_copy(out=ident_bf[:], in_=ident[:])
+        off_runs = off[:].rearrange("p j (k i) -> p j k i", i=J)
+        off_wide = const.tile([P, 2, P // J, 2 * J], BF16, name="off_wide")
+        nc.vector.memset(off_wide[:], 1.0)
+        for j in range(2):
+            nc.vector.tensor_copy(out=off_wide[:, j, :, j * J : (j + 1) * J], in_=off_runs[:, j])
+        rec = const.tile([P, J, T * E], F32, name="rec")
+        neg_rec = const.tile([P, J, T * E], F32, name="neg_rec")
+
+        def reciprocals():
+            nc.vector.tensor_copy(
+                out=den_sorted[0 : T * E, :].rearrange("r (j k i) -> r j k i", j=J, i=J),
+                in_=den_rows[:].rearrange("r (k j i) -> r j k i", j=J, i=J),
+            )
+            den_bank = psum.tile([P, J, P], F32, name="turn_bank", tag="bank", bufs=4)
+            for j in range(J):
+                nc.tensor.transpose(den_bank[:, j, :], den_sorted[:, j * P : (j + 1) * P], ident[:])
+            nc.vector.reciprocal(out=rec[:], in_=den_bank[:, :, 0 : T * E])
+            nc.vector.tensor_scalar(out=neg_rec[:], in0=rec[:], scalar1=-1.0, scalar2=None, op0=ALU.mult)
+
+        w_g, w_q, dz2_t, dz2_g, dz2_q, nf_g, nf_q = {}, {}, {}, {}, {}, {}, {}
+        masked_g, masked_q, sign_t, dz1_t, dz1n_g, dz1n_q, dz1d_g, dz1d_q = {}, {}, {}, {}, {}, {}, {}, {}
+        result_t, neg_r_t, dm_t = {}, {}, {}
+
+        def group_w(c, engine):
+            w_g[c] = grouped_tile()
+            interleave(
+                engine,
+                w_raw[c][:].rearrange("p (j q u e) -> p q j u e", j=J, u=2, e=2),
+                w_g[c][:].rearrange("p (u q e j) -> p q j u e", u=2, e=2, j=J),
+            )
+
+        def quantize_w(c):
+            w_q[c] = quantize(w_g[c], E4, "w", 3)
+
+        def slope_factor(t, cols):
+            nc.vector.tensor_scalar(out=z_t[t][:, cols], in0=z_t[t][:, cols], scalar1=0.0, scalar2=SLOPE, op0=ALU.is_ge, op1=ALU.max)
+
+        def make_dz2(t, cols):
+            if t not in dz2_t:
+                dz2_t[t] = work.tile([P, J * W], BF16, name="dz2", tag="dz2")
+            nc.vector.tensor_tensor(out=dz2_t[t][:, cols], in0=g_t[t][:, cols], in1=z_t[t][:, cols], op=ALU.mult)
+
+        def turn_dz2(t):
+            dz2_g[t] = turn(dz2_t[t], every_second)
+
+        def quantize_dz2(t):
+            dz2_q[t] = quantize(dz2_g[t], E5, "dz2", 3)
+
+        def turn_nf(t):
+            nf_g[t] = turn(nf_t[t], every_second)
+
+        def quantize_nf(t):
+            nf_q[t] = quantize(nf_g[t], E4, "nf", 2)
+
+        def mask_edge(s):
+            runs = edge_t[s][:].rearrange("p (h j k y) -> p h j k y", h=2, j=2, y=16)
+            for h in range(2):
+                part = runs[:, h, :, :, 8 * h : 8 * h + 8]
+                nc.vector.tensor_tensor(out=part, in0=part, in1=off_wide[:], op=ALU.mult)
+
+        def group_edge(s, engine):
+            masked_g[s] = grouped_tile()
+            interleave(
+                engine,
+                edge_t[s][:].rearrange("p (n k j i) -> p j k n i", n=J, j=J, i=J),
+                masked_g[s][:].rearrange("p (j k i n) -> p j k n i", n=J, j=J, i=J),
+            )
+
+        def quantize_edge(s):
+            masked_q[s] = quantize(masked_g[s], E4, "masked", 4)
+
+        def sign_edge(s):
+            sign_t[s] = work.tile([P, J * W], BF16, name="sign", tag="sign", bufs=3)
+            nc.scalar.activation(out=sign_t[s][:], in_=edge_t[s][:], func=ACT.Sign)
+
+        def sign_edge_split(s, n):
+            sign_t[s] = work.tile([P, J * W], BF16, name="sign", tag="sign", bufs=3)
+            if n > 0:
+                nc.scalar.activation(out=sign_t[s][:, 0:n], in_=edge_t[s][:, 0:n], func=ACT.Sign)
+
+        def sign_edge_rest(s, n):
+            if n < J * W:
+                nc.vector.tensor_scalar(out=sign_t[s][:, n:], in0=edge_t[s][:, n:], scalar1=2.0**34, scalar2=2.0**-100, op0=ALU.mult, op1=ALU.min)
+
+        def sign_edge_rest2(s, n):
+            if n < J * W:
+                nc.vector.tensor_scalar(out=sign_t[s][:, n:], in0=sign_t[s][:, n:], scalar1=-(2.0**-100), scalar2=2.0**100, op0=ALU.max, op1=ALU.mult)
+
+        def make_dz1(s, j):
+            if j == 0:
+                dz1_t[s] = work.tile([P, J * W], BF16, name="dz1", tag="dz1", bufs=2)
+            bank = psum.tile([P, W], F32, name="mm_bank", tag="bank", bufs=4)
+            mx_pass(bank, dz2_q[s // E], j, w_q[1 + s % E], True, True)
+            nc.scalar.activation(out=dz1_t[s][:, j * W : (j + 1) * W], in_=bank[:], func=ACT.Copy, scale=rec[:, j, s : s + 1])
+
+        def turn_dz1(s):
+            dz1d_g[s] = turn(dz1_t[s], contiguous)
+
+        def quantize_dz1d(s):
+            dz1d_q[s] = quantize(dz1d_g[s], E5, "dz1d", 2)
+
+        def group_dz1(s, engine):
+            dz1n_g[s] = grouped_tile()
+            interleave(
+                engine,
+                dz1_t[s][:].rearrange("p (j c i) -> p c j i", j=J, i=J),
+                dz1n_g[s][:].rearrange("p (c i j) -> p c j i", j=J, i=J),
+            )
+
+        def move_dz1(s):
+            dz1n_g[s] = grouped_tile()
+            src = dz1_t[s][:].rearrange("p (j c) -> p c j", j=J)
+            for half in range(2):
+                bank = psum.tile([P, 2, W], BF16, name="turn_bank", tag="bank", bufs=4)
+                for q in range(2):
+                    c0 = (2 * half + q) * P
+                    nc.tensor.matmul(bank[:, q, :].rearrange("p (c j) -> p c j", j=J), lhsT=ident_bf[:], rhs=src[:, c0 : c0 + P, :], start=True, stop=True)
+                nc.scalar.copy(out=dz1n_g[s][:, half * 2 * W : (half + 1) * 2 * W], in_=bank[:].rearrange("p q w -> p (q w)"))
+
+        def quantize_dz1n(s):
+            dz1n_q[s] = quantize(dz1n_g[s], E5, "dz1n", 3)
+
+        def make_dm(s, j):
+            dm_t[s, j] = psum.tile([P, W], F32, name="dm_bank", tag="dm_bank", bufs=4)
+            mx_pass(dm_t[s, j], dz1d_q[s], j, nf_q[s // E], True, True)
+
+        def row_sum(s, j):
+            if j == 0:
+                result_t[s] = work.tile([P, PADDED], F32, name="edge_grad", tag="edge_grad", bufs=3)
+                neg_r_t[s] = work.tile([P, J], F32, name="neg_r", tag="neg_r", bufs=3)
+            products = work.tile([P, W], F32, name="products", tag="products", bufs=2)
+            nc.vector.scalar_tensor_tensor(
+                out=products[:],
+                in0=dm_t[s, j][:],
+                scalar=neg_rec[:, j, s : s + 1],
+                in1=edge_t[s][:, j * W : (j + 1) * W],
+                op0=ALU.mult,
+                op1=ALU.mult,
+                accum_out=neg_r_t[s][:, j : j + 1],
+            )
+
+        def finish(s, j):
+            nc.vector.scalar_tensor_tensor(
+                out=result_t[s][:, j * W : (j + 1) * W],
+                in0=sign_t[s][:, j * W : (j + 1) * W],
+                scalar=neg_r_t[s][:, j : j + 1],
+                in1=dm_t[s, j][:],
+                op0=ALU.mult,
+                op1=ALU.add,
+            )
+
+        def store_edge_gradient(s, engine, js):
+            runs = diagonal_runs(result_t[s])[:, js]
+            engine.tensor_tensor(out=runs, in0=runs, in1=off_runs[:, js], op=ALU.mult)
+            store_nodes(out_1[s // E, s % E], result_t[s], js)
+
+        def node_gradient(t):
+            result = work.tile([P, J * W], F32, name="node_grad", tag="node_grad", bufs=2)
+            for j in range(J):
+                bank = psum.tile([P, W], F32, name="mm_bank", tag="bank", bufs=4)
+                mx_pass(bank, dz2_q[t], j, w_q[0], True, False)
+                mx_pass(bank, masked_q[E * t], j, dz1n_q[E * t], False, False)
+                mx_pass(bank, masked_q[E * t + 1], j, dz1n_q[E * t + 1], False, True)
+                nc.scalar.copy(
+                    out=result[:, j * W : (j + 1) * W].rearrange("p (q u e) -> p q u e", u=2, e=2),
+                    in_=bank[:].rearrange("p (u q e) -> p q u e", u=2, e=2),
+                )
+            store_nodes(out_0[t], result, slice(0, J))
+
+        whole = slice(0, J * W)
+        halves = [slice(0, 2 * W), slice(2 * W, J * W)]
+
+        group_w(1, "vector")
+        mask_edge(0)
+        sign_edge(0)
+        group_edge(0, "scalar")
+        quantize_w(1)
+        reciprocals()
+        for cols in halves:
+            slope_factor(0, cols)
+        for cols in halves:
+            make_dz2(0, cols)
+        turn_dz2(0)
+        turn_nf(0)
+        group_w(2, "vector")
+        quantize_dz2(0)
+        quantize_edge(0)
+        quantize_nf(0)
+        quantize_w(2)
+
+        last = T * E
+        for s in range(last + 1):
+            t, e = divmod(s, E)
+            more = t + 1 < T
+            if False and 0 < s < last:
+                group_edge(s, "gpsimd")
+                if s > 1:
+                    store_edge_gradient(s - 2, nc.gpsimd, slice(0, J))
+            if s < last:
+                for j in range(J):
+                    make_dz1(s, j)
+                turn_dz1(s)
+            if s > 0:
+                if s == last:
+                    node_gradient(t - 1)
+                row_sum(s - 1, 0)
+                row_sum(s - 1, 1)
+                finish(s - 1, 0)
+                row_sum(s - 1, 2)
+                finish(s - 1, 1)
+                row_sum(s - 1, 3)
+                if s == last:
+                    store_edge_gradient(s - 1, nc.vector, slice(0, 2))
+                finish(s - 1, 2)
+                finish(s - 1, 3)
+            if s == last:
+                store_edge_gradient(s - 1, nc.vector, slice(2, J))
+                break
+            if e == 1 and more:
+                turn_dz2(t + 1)
+                turn_nf(t + 1)
+            n_sign = 2048 if e == 0 else 2048
+            if s == last - 1:
+                n_sign = J * W
+            if s == 0:
+                group_w(0, "vector")
+                slope_factor(t + 1, whole)
+                quantize_w(0)
+            if e == 1 and more:
+                quantize_dz2(t + 1)
+            quantize_dz1d(s)
+            for j in range(J):
+                make_dm(s, j)
+            if s > 0:
+                if not False:
+                    group_edge(s, "vector" if e == 0 else "both")
+                sign_edge_split(s, n_sign)
+            group_dz1(s, "vector" if s == last - 1 else ("scalar" if e == 0 else "scalar"))
+            if s > 0:
+                quantize_dz1n(s - 1)
+                if not False or s == last - 1:
+                    store_edge_gradient(s - 1, nc.vector, slice(0, J))
+                sign_edge_rest(s, n_sign)
+                quantize_edge(s)
+                sign_edge_rest2(s, n_sign)
+            if e == 0:
+                if t > 0:
+                    node_gradient(t - 1)
+                if more:
+                    if s > 0:
+                        slope_factor(t + 1, whole)
+                    make_dz2(t + 1, whole)
+                mask_edge(s + 1)
+                if t + 2 < T:
+                    load_gz(t + 2)
+            else:
+                if more:
+                    quantize_nf(t + 1)
+                    mask_edge(s + 1)
+                else:
+                    quantize_dz1n(s)
+                if t + 2 < T:
+                    load_nf(t + 2)
+            if s + 4 < last:
+                load_edge(s + 4)

@@ -136,14 +136,14 @@ def tile_nodeupdatenetwork_pa_v_kernel(tc, node_feat, edge_feat, w0, denom, z, g
         ctx.enter_context(tc.manual_schedule())
 
         den_rows = const.tile([T * E, N], F32, name="den_rows")
-        load_w(1)
         nc.sync.dma_start(out=den_rows[:], in_=denom.rearrange("t e n -> (t e) n"))
-        load_edge(0)
+        load_w(1)
         load_gz(0)
+        load_edge(0)
         load_nf(0)
         load_w(2)
-        load_edge(1)
         load_w(0)
+        load_edge(1)
         load_gz(1)
         load_nf(1)
         load_edge(2)
@@ -155,8 +155,6 @@ def tile_nodeupdatenetwork_pa_v_kernel(tc, node_feat, edge_feat, w0, denom, z, g
         off = const.tile([P, J, P], BF16, name="off")
         for j in range(J):
             nc.vector.tensor_scalar(out=off[:, j, :], in0=ident[:], scalar1=-1.0, scalar2=1.0, op0=ALU.mult, op1=ALU.add)
-        ident_bf = const.tile([P, P], BF16, name="ident_bf")
-        nc.vector.tensor_copy(out=ident_bf[:], in_=ident[:])
         off_runs = off[:].rearrange("p j (k i) -> p j k i", i=J)
         off_wide = const.tile([P, 2, P // J, 2 * J], BF16, name="off_wide")
         nc.vector.memset(off_wide[:], 1.0)
@@ -165,7 +163,7 @@ def tile_nodeupdatenetwork_pa_v_kernel(tc, node_feat, edge_feat, w0, denom, z, g
         rec = const.tile([P, J, T * E], F32, name="rec")
         neg_rec = const.tile([P, J, T * E], F32, name="neg_rec")
 
-        def reciprocals():
+        def turn_denominators():
             nc.vector.tensor_copy(
                 out=den_sorted[0 : T * E, :].rearrange("r (j k i) -> r j k i", j=J, i=J),
                 in_=den_rows[:].rearrange("r (k j i) -> r j k i", j=J, i=J),
@@ -173,6 +171,9 @@ def tile_nodeupdatenetwork_pa_v_kernel(tc, node_feat, edge_feat, w0, denom, z, g
             den_bank = psum.tile([P, J, P], F32, name="turn_bank", tag="bank", bufs=4)
             for j in range(J):
                 nc.tensor.transpose(den_bank[:, j, :], den_sorted[:, j * P : (j + 1) * P], ident[:])
+            return den_bank
+
+        def reciprocals(den_bank):
             nc.vector.reciprocal(out=rec[:], in_=den_bank[:, :, 0 : T * E])
             nc.vector.tensor_scalar(out=neg_rec[:], in0=rec[:], scalar1=-1.0, scalar2=None, op0=ALU.mult)
 
@@ -245,12 +246,16 @@ def tile_nodeupdatenetwork_pa_v_kernel(tc, node_feat, edge_feat, w0, denom, z, g
             if n < J * W:
                 nc.vector.tensor_scalar(out=sign_t[s][:, n:], in0=sign_t[s][:, n:], scalar1=-(2.0**-100), scalar2=2.0**100, op0=ALU.max, op1=ALU.mult)
 
+        dx_t, node_t = {}, {}
+
+        def make_dx(s, j):
+            dx_t[s, j] = psum.tile([P, W], F32, name="bank", tag="bank", bufs=4)
+            mx_pass(dx_t[s, j], dz2_q[s // E], j, w_q[1 + s % E], True, True)
+
         def make_dz1(s, j):
             if j == 0:
                 dz1_t[s] = work.tile([P, J * W], BF16, name="dz1", tag="dz1", bufs=2)
-            bank = psum.tile([P, W], F32, name="mm_bank", tag="bank", bufs=4)
-            mx_pass(bank, dz2_q[s // E], j, w_q[1 + s % E], True, True)
-            nc.scalar.activation(out=dz1_t[s][:, j * W : (j + 1) * W], in_=bank[:], func=ACT.Copy, scale=rec[:, j, s : s + 1])
+            nc.scalar.activation(out=dz1_t[s][:, j * W : (j + 1) * W], in_=dx_t[s, j][:], func=ACT.Copy, scale=rec[:, j, s : s + 1])
 
         def turn_dz1(s):
             dz1d_g[s] = turn(dz1_t[s], contiguous)
@@ -266,18 +271,8 @@ def tile_nodeupdatenetwork_pa_v_kernel(tc, node_feat, edge_feat, w0, denom, z, g
                 dz1n_g[s][:].rearrange("p (c i j) -> p c j i", j=J, i=J),
             )
 
-        def move_dz1(s):
-            dz1n_g[s] = grouped_tile()
-            src = dz1_t[s][:].rearrange("p (j c) -> p c j", j=J)
-            for half in range(2):
-                bank = psum.tile([P, 2, W], BF16, name="turn_bank", tag="bank", bufs=4)
-                for q in range(2):
-                    c0 = (2 * half + q) * P
-                    nc.tensor.matmul(bank[:, q, :].rearrange("p (c j) -> p c j", j=J), lhsT=ident_bf[:], rhs=src[:, c0 : c0 + P, :], start=True, stop=True)
-                nc.scalar.copy(out=dz1n_g[s][:, half * 2 * W : (half + 1) * 2 * W], in_=bank[:].rearrange("p q w -> p (q w)"))
-
         def quantize_dz1n(s):
-            dz1n_q[s] = quantize(dz1n_g[s], E5, "dz1n", 3)
+            dz1n_q[s] = quantize(dz1n_g[s], E5, "dz1n", 4)
 
         def make_dm(s, j):
             dm_t[s, j] = psum.tile([P, W], F32, name="dm_bank", tag="dm_bank", bufs=4)
@@ -313,55 +308,66 @@ def tile_nodeupdatenetwork_pa_v_kernel(tc, node_feat, edge_feat, w0, denom, z, g
             engine.tensor_tensor(out=runs, in0=runs, in1=off_runs[:, js], op=ALU.mult)
             store_nodes(out_1[s // E, s % E], result_t[s], js)
 
-        def node_gradient(t):
-            result = work.tile([P, J * W], F32, name="node_grad", tag="node_grad", bufs=2)
-            for j in range(J):
-                bank = psum.tile([P, W], F32, name="mm_bank", tag="bank", bufs=4)
+        def node_gradient(t, js):
+            if js.start == 0:
+                node_t[t] = work.tile([P, J * W], F32, name="node_grad", tag="node_grad", bufs=2)
+            for j in range(js.start, js.stop):
+                bank = psum.tile([P, W], F32, name="bank", tag="bank", bufs=4)
                 mx_pass(bank, dz2_q[t], j, w_q[0], True, False)
                 mx_pass(bank, masked_q[E * t], j, dz1n_q[E * t], False, False)
                 mx_pass(bank, masked_q[E * t + 1], j, dz1n_q[E * t + 1], False, True)
                 nc.scalar.copy(
-                    out=result[:, j * W : (j + 1) * W].rearrange("p (q u e) -> p q u e", u=2, e=2),
+                    out=node_t[t][:, j * W : (j + 1) * W].rearrange("p (q u e) -> p q u e", u=2, e=2),
                     in_=bank[:].rearrange("p (u q e) -> p q u e", u=2, e=2),
                 )
-            store_nodes(out_0[t], result, slice(0, J))
+
+        def store_node_gradient(t, js):
+            store_nodes(out_0[t], node_t[t], js)
 
         whole = slice(0, J * W)
         halves = [slice(0, 2 * W), slice(2 * W, J * W)]
 
+        den_bank = turn_denominators()
         group_w(1, "vector")
-        mask_edge(0)
-        sign_edge(0)
-        group_edge(0, "scalar")
+        reciprocals(den_bank)
         quantize_w(1)
-        reciprocals()
         for cols in halves:
             slope_factor(0, cols)
         for cols in halves:
             make_dz2(0, cols)
         turn_dz2(0)
         turn_nf(0)
-        group_w(2, "vector")
+        mask_edge(0)
+        group_edge(0, "vector")
         quantize_dz2(0)
+        for j in range(J):
+            make_dx(0, j)
         quantize_edge(0)
+        group_w(2, "vector")
         quantize_nf(0)
         quantize_w(2)
+        group_w(0, "vector")
 
         last = T * E
         for s in range(last + 1):
             t, e = divmod(s, E)
             more = t + 1 < T
-            if False and 0 < s < last:
+            if True and 0 < s < last:
                 group_edge(s, "gpsimd")
                 if s > 1:
                     store_edge_gradient(s - 2, nc.gpsimd, slice(0, J))
             if s < last:
                 for j in range(J):
                     make_dz1(s, j)
+                if e == 1 and more:
+                    turn_dz2(t + 1)
                 turn_dz1(s)
             if s > 0:
                 if s == last:
-                    node_gradient(t - 1)
+                    node_gradient(t - 1, slice(0, 2))
+                    store_node_gradient(t - 1, slice(0, 2))
+                    node_gradient(t - 1, slice(2, J))
+                    store_node_gradient(t - 1, slice(2, J))
                 row_sum(s - 1, 0)
                 row_sum(s - 1, 1)
                 finish(s - 1, 0)
@@ -375,39 +381,54 @@ def tile_nodeupdatenetwork_pa_v_kernel(tc, node_feat, edge_feat, w0, denom, z, g
             if s == last:
                 store_edge_gradient(s - 1, nc.vector, slice(2, J))
                 break
-            if e == 1 and more:
-                turn_dz2(t + 1)
-                turn_nf(t + 1)
             n_sign = 2048 if e == 0 else 2048
-            if s == last - 1:
-                n_sign = J * W
+            if not more:
+                n_sign = 2048 if e == 0 else 2048
             if s == 0:
-                group_w(0, "vector")
-                slope_factor(t + 1, whole)
-                quantize_w(0)
+                sign_edge(0)
             if e == 1 and more:
                 quantize_dz2(t + 1)
-            quantize_dz1d(s)
-            for j in range(J):
-                make_dm(s, j)
-            if s > 0:
-                if not False:
-                    group_edge(s, "vector" if e == 0 else "both")
-                sign_edge_split(s, n_sign)
-            group_dz1(s, "vector" if s == last - 1 else ("scalar" if e == 0 else "scalar"))
             if s > 0:
                 quantize_dz1n(s - 1)
-                if not False or s == last - 1:
+                if s == last - 1:
+                    store_edge_gradient(s - 1, nc.vector, slice(0, J))
+                if not True:
+                    group_edge(s, "undefined" if e == 0 else "undefined")
+                sign_edge_split(s, n_sign)
+                if e == 1 and more:
+                    turn_nf(t + 1)
+            if e == 1 and t > 0 and False:
+                node_gradient(t - 1, slice(2, J))
+                store_node_gradient(t - 1, slice(0, J))
+            quantize_dz1d(s)
+            if e == 0 and t > 0:
+                node_gradient(t - 1, slice(0, 2 if False else J))
+                if not False:
+                    store_node_gradient(t - 1, slice(0, J))
+            if True:
+                for j in range(J):
+                    make_dm(s, j)
+            if s + 1 < last:
+                for j in range(J):
+                    make_dx(s + 1, j)
+            if not True:
+                for j in range(J):
+                    make_dm(s, j)
+            group_dz1(s, ("vector" if e == 0 else "vector") if not more else ("both" if e == 0 else "scalar"))
+            if s > 0:
+                if not True:
                     store_edge_gradient(s - 1, nc.vector, slice(0, J))
                 sign_edge_rest(s, n_sign)
-                quantize_edge(s)
+                if e == 1 or not more:
+                    quantize_edge(s)
                 sign_edge_rest2(s, n_sign)
             if e == 0:
-                if t > 0:
-                    node_gradient(t - 1)
                 if more:
-                    if s > 0:
-                        slope_factor(t + 1, whole)
+                    slope_factor(t + 1, whole)
+                    if s == 0:
+                        quantize_w(0)
+                    else:
+                        quantize_edge(s)
                     make_dz2(t + 1, whole)
                 mask_edge(s + 1)
                 if t + 2 < T:

@@ -102,9 +102,9 @@ def tile_nodeupdatenetwork_pa_v_kernel(tc, node_feat, edge_feat, w0, denom, z, g
         def interleave(engine, src, dst):
             if engine == "gpsimd":
                 for a in range(4):
-                    n = src.shape[1] // 4
-                    s1 = src[:, a] if n == 1 else src[:, a * n : (a + 1) * n]
-                    d1 = dst[:, a] if n == 1 else dst[:, a * n : (a + 1) * n]
+                    n = 1
+                    s1 = src[:, a].rearrange("p k n i -> p k i n")
+                    d1 = dst[:, a].rearrange("p k n i -> p k i n")
                     nc.gpsimd.tensor_scalar(out=d1, in0=s1, scalar1=1.0, scalar2=0.0, op0=ALU.mult, op1=ALU.add)
             elif engine == "both":
                 n = src.shape[1] // 2
@@ -138,8 +138,8 @@ def tile_nodeupdatenetwork_pa_v_kernel(tc, node_feat, edge_feat, w0, denom, z, g
         den_rows = const.tile([T * E, N], F32, name="den_rows")
         nc.sync.dma_start(out=den_rows[:], in_=denom.rearrange("t e n -> (t e) n"))
         load_w(1)
-        load_gz(0)
         load_edge(0)
+        load_gz(0)
         load_nf(0)
         load_w(2)
         load_w(0)
@@ -179,7 +179,7 @@ def tile_nodeupdatenetwork_pa_v_kernel(tc, node_feat, edge_feat, w0, denom, z, g
 
         w_g, w_q, dz2_t, dz2_g, dz2_q, nf_g, nf_q = {}, {}, {}, {}, {}, {}, {}
         masked_g, masked_q, sign_t, dz1_t, dz1n_g, dz1n_q, dz1d_g, dz1d_q = {}, {}, {}, {}, {}, {}, {}, {}
-        result_t, neg_r_t, dm_t = {}, {}, {}
+        result_t, neg_r_t, dm_t, moved_t = {}, {}, {}, {}
 
         def group_w(c, engine):
             w_g[c] = grouped_tile()
@@ -329,6 +329,9 @@ def tile_nodeupdatenetwork_pa_v_kernel(tc, node_feat, edge_feat, w0, denom, z, g
 
         den_bank = turn_denominators()
         group_w(1, "vector")
+        mask_edge(0)
+        sign_edge(0)
+        group_edge(0, "scalar")
         reciprocals(den_bank)
         quantize_w(1)
         for cols in halves:
@@ -337,24 +340,24 @@ def tile_nodeupdatenetwork_pa_v_kernel(tc, node_feat, edge_feat, w0, denom, z, g
             make_dz2(0, cols)
         turn_dz2(0)
         turn_nf(0)
-        mask_edge(0)
-        group_edge(0, "vector")
+        group_w(2, "vector")
+        quantize_edge(0)
         quantize_dz2(0)
         for j in range(J):
             make_dx(0, j)
-        quantize_edge(0)
-        group_w(2, "vector")
-        quantize_nf(0)
         quantize_w(2)
         group_w(0, "vector")
+        quantize_nf(0)
+        slope_factor(1, whole)
+        make_dz2(1, whole)
 
         last = T * E
         for s in range(last + 1):
             t, e = divmod(s, E)
             more = t + 1 < T
-            if True and 0 < s < last:
+            if 0 < s < last:
                 group_edge(s, "gpsimd")
-                if s > 1:
+                if s > 1 and True:
                     store_edge_gradient(s - 2, nc.gpsimd, slice(0, J))
             if s < last:
                 for j in range(J):
@@ -381,64 +384,65 @@ def tile_nodeupdatenetwork_pa_v_kernel(tc, node_feat, edge_feat, w0, denom, z, g
             if s == last:
                 store_edge_gradient(s - 1, nc.vector, slice(2, J))
                 break
-            n_sign = 2048 if e == 0 else 2048
-            if not more:
-                n_sign = 2048 if e == 0 else 2048
             if s == 0:
-                sign_edge(0)
-            if e == 1 and more:
-                quantize_dz2(t + 1)
-            if s > 0:
-                quantize_dz1n(s - 1)
-                if s == last - 1:
-                    store_edge_gradient(s - 1, nc.vector, slice(0, J))
-                if not True:
-                    group_edge(s, "undefined" if e == 0 else "undefined")
-                sign_edge_split(s, n_sign)
-                if e == 1 and more:
-                    turn_nf(t + 1)
-            if e == 1 and t > 0 and False:
-                node_gradient(t - 1, slice(2, J))
-                store_node_gradient(t - 1, slice(0, J))
-            quantize_dz1d(s)
-            if e == 0 and t > 0:
-                node_gradient(t - 1, slice(0, 2 if False else J))
-                if not False:
-                    store_node_gradient(t - 1, slice(0, J))
-            if True:
-                for j in range(J):
-                    make_dm(s, j)
-            if s + 1 < last:
                 for j in range(J):
                     make_dx(s + 1, j)
-            if not True:
+                quantize_dz1d(s)
                 for j in range(J):
                     make_dm(s, j)
-            group_dz1(s, ("vector" if e == 0 else "vector") if not more else ("both" if e == 0 else "scalar"))
-            if s > 0:
+                group_dz1(s, "scalar")
+                quantize_w(0)
+                mask_edge(1)
+                load_gz(2)
+            elif s == last - 1:
+                quantize_dz1d(s)
+                for j in range(J):
+                    make_dm(s, j)
+                group_dz1(s, "both")
+                sign_edge(s)
+                store_edge_gradient(s - 1, nc.vector, slice(0, J))
+                quantize_dz1n(s - 1)
+                quantize_edge(s)
+                quantize_dz1n(s)
+            elif e == 0:
+                quantize_dz1n(s - 1)
+                sign_edge(s)
+                quantize_dz1d(s)
                 if not True:
                     store_edge_gradient(s - 1, nc.vector, slice(0, J))
-                sign_edge_rest(s, n_sign)
-                if e == 1 or not more:
-                    quantize_edge(s)
-                sign_edge_rest2(s, n_sign)
-            if e == 0:
+                node_gradient(t - 1, slice(0, J))
+                store_node_gradient(t - 1, slice(0, J))
+                for j in range(J):
+                    make_dm(s, j)
+                for j in range(J):
+                    make_dx(s + 1, j)
+                group_dz1(s, "both" if more else "vector")
                 if more:
                     slope_factor(t + 1, whole)
-                    if s == 0:
-                        quantize_w(0)
-                    else:
-                        quantize_edge(s)
+                quantize_edge(s)
+                if more:
                     make_dz2(t + 1, whole)
                 mask_edge(s + 1)
                 if t + 2 < T:
                     load_gz(t + 2)
             else:
-                if more:
-                    quantize_nf(t + 1)
-                    mask_edge(s + 1)
-                else:
-                    quantize_dz1n(s)
+                quantize_dz2(t + 1)
+                quantize_dz1n(s - 1)
+                sign_edge(s)
+                turn_nf(t + 1)
+                quantize_dz1d(s)
+                if not True:
+                    store_edge_gradient(s - 1, nc.vector, slice(0, J))
+                for j in range(J):
+                    make_dm(s, j)
+                for j in range(J):
+                    make_dx(s + 1, j)
+                group_dz1(s, "scalar")
+                quantize_edge(s)
+                if s == 1 and False:
+                    quantize_w(0)
+                quantize_nf(t + 1)
+                mask_edge(s + 1)
                 if t + 2 < T:
                     load_nf(t + 2)
             if s + 4 < last:

@@ -102,14 +102,18 @@ def tile_nodeupdatenetwork_pa_v_kernel(tc, node_feat, edge_feat, w0, denom, z, g
         def interleave(engine, src, dst):
             if engine == "gpsimd":
                 for a in range(4):
-                    n = 1
-                    s1 = src[:, a].rearrange("p k n i -> p k i n")
-                    d1 = dst[:, a].rearrange("p k n i -> p k i n")
+                    n = src.shape[1] // 4
+                    s1 = src[:, a] if n == 1 else src[:, a * n : (a + 1) * n]
+                    d1 = dst[:, a] if n == 1 else dst[:, a * n : (a + 1) * n]
                     nc.gpsimd.tensor_scalar(out=d1, in0=s1, scalar1=1.0, scalar2=0.0, op0=ALU.mult, op1=ALU.add)
             elif engine == "both":
                 n = src.shape[1] // 2
                 nc.scalar.copy(out=dst[:, 0:n], in_=src[:, 0:n])
                 nc.vector.tensor_copy(out=dst[:, n : 2 * n], in_=src[:, n : 2 * n])
+            elif engine[0] == "s" and engine != "scalar":
+                n = int(engine[1:])
+                nc.scalar.copy(out=dst[:, 0:n], in_=src[:, 0:n])
+                nc.vector.tensor_copy(out=dst[:, n:], in_=src[:, n:])
             else:
                 copy_on(engine, dst, src)
 
@@ -154,7 +158,7 @@ def tile_nodeupdatenetwork_pa_v_kernel(tc, node_feat, edge_feat, w0, denom, z, g
         nc.gpsimd.memset(den_sorted[:], 1.0)
         off = const.tile([P, J, P], BF16, name="off")
         for j in range(J):
-            nc.vector.tensor_scalar(out=off[:, j, :], in0=ident[:], scalar1=-1.0, scalar2=1.0, op0=ALU.mult, op1=ALU.add)
+            nc.scalar.activation(out=off[:, j, :], in_=ident[:], func=ACT.Sign, scale=-1.0, bias=1.0)
         off_runs = off[:].rearrange("p j (k i) -> p j k i", i=J)
         off_wide = const.tile([P, 2, P // J, 2 * J], BF16, name="off_wide")
         nc.vector.memset(off_wide[:], 1.0)
@@ -357,7 +361,7 @@ def tile_nodeupdatenetwork_pa_v_kernel(tc, node_feat, edge_feat, w0, denom, z, g
             more = t + 1 < T
             if 0 < s < last:
                 group_edge(s, "gpsimd")
-                if s > 1 and True:
+                if s > 1 and False:
                     store_edge_gradient(s - 2, nc.gpsimd, slice(0, J))
             if s < last:
                 for j in range(J):
@@ -408,7 +412,7 @@ def tile_nodeupdatenetwork_pa_v_kernel(tc, node_feat, edge_feat, w0, denom, z, g
                 quantize_dz1n(s - 1)
                 sign_edge(s)
                 quantize_dz1d(s)
-                if not True:
+                if not False:
                     store_edge_gradient(s - 1, nc.vector, slice(0, J))
                 node_gradient(t - 1, slice(0, J))
                 store_node_gradient(t - 1, slice(0, J))
@@ -431,7 +435,7 @@ def tile_nodeupdatenetwork_pa_v_kernel(tc, node_feat, edge_feat, w0, denom, z, g
                 sign_edge(s)
                 turn_nf(t + 1)
                 quantize_dz1d(s)
-                if not True:
+                if not False:
                     store_edge_gradient(s - 1, nc.vector, slice(0, J))
                 for j in range(J):
                     make_dm(s, j)

@@ -20,8 +20,14 @@ ACT = mybir.ActivationFunctionType
 P = 128
 J = 4
 W = 512
+GROUP = J * J
 SKEW = W + J
 PADDED = J * SKEW
+STEPS = T * E
+
+GROUPED_BUFS = 7
+EDGE_BUFS = 5
+BANK_BUFS = 4
 
 
 def tile_nodeupdatenetwork_pa_v_kernel(tc, node_feat, edge_feat, w0, denom, z, grad_out, out_0, out_1):
@@ -34,22 +40,27 @@ def tile_nodeupdatenetwork_pa_v_kernel(tc, node_feat, edge_feat, w0, denom, z, g
         quant = ctx.enter_context(tc.tile_pool(name="quant", bufs=2))
         psum = ctx.enter_context(tc.psum_pool(name="psum", bufs=1))
 
-        def node_rows(rows, i):
-            return rows.rearrange("(k j i) w -> i k j w", j=J, i=J)[i]
 
-        def slots(buf):
+        def node_rows(matrix, i):
+            return matrix.rearrange("(k j i) w -> i k j w", j=J, i=J)[i]
+
+        def rows_of(buf):
             return buf[:, 0 : J * W].rearrange("p (j w) -> p j w", j=J)
 
-        def load_nodes(buf, rows):
+        def load_nodes(buf, matrix):
             for i in range(J):
-                nc.sync.dma_start(out=slots(buf)[i:P:J], in_=node_rows(rows, i))
+                nc.sync.dma_start(out=rows_of(buf)[i:P:J], in_=node_rows(matrix, i))
 
-        def store_nodes(rows, buf, js):
+        def store_nodes(matrix, buf, js):
             for i in range(J):
-                nc.sync.dma_start(out=node_rows(rows, i)[:, js], in_=slots(buf)[i:P:J, js])
+                nc.sync.dma_start(out=node_rows(matrix, i)[:, js], in_=rows_of(buf)[i:P:J, js])
 
         def diagonal_runs(buf):
-            return buf[:].rearrange("p (j x) -> p j x", x=SKEW)[:, :, 0:W].rearrange("p j (k y) -> p j k y", y=16)[:, :, :, 0:J]
+            skewed = buf[:].rearrange("p (j x) -> p j x", x=SKEW)[:, :, 0:W]
+            return skewed.rearrange("p j (k y) -> p j k y", y=GROUP)[:, :, :, 0:J]
+
+        def grouped_tile():
+            return work.tile([P, J * W], BF16, name="grouped", tag="grouped", bufs=GROUPED_BUFS, align_bytes=64)
 
         def quantize(grouped, fmt, tag, bufs):
             codes = quant.tile([P, W], U32, name=tag + "_codes", tag=tag + "_codes", bufs=bufs, align_bytes=64)
@@ -69,53 +80,39 @@ def tile_nodeupdatenetwork_pa_v_kernel(tc, node_feat, edge_feat, w0, denom, z, g
                 stop=stop,
             )
 
-        def grouped_tile():
-            return work.tile([P, J * W], BF16, name="grouped", tag="grouped", bufs=7, align_bytes=64)
-
-        def copy_on(engine, out, in_):
-            if engine == "vector":
-                nc.vector.tensor_copy(out=out, in_=in_)
-            else:
-                nc.scalar.copy(out=out, in_=in_)
-
-        def turn_half(rows, word_block, grouped, half):
-            words = rows[:, 0 : J * W].bitcast(F32).rearrange("p (j w) -> p j w", j=J)
-            dst = grouped[:].bitcast(F32).rearrange("q (j p u) -> q j p u", j=J, u=2)
-            bank = psum.tile([P, 2, 2, P], F32, name="turn_bank", tag="bank", bufs=4)
-            for jj in range(2):
-                for u in range(2):
-                    nc.tensor.transpose(bank[:, jj, u, :], word_block(words[:, 2 * half + jj, :], u), ident[:])
-            nc.scalar.copy(out=dst[:, 2 * half : 2 * half + 2], in_=bank[:].rearrange("q j u p -> q j p u"))
-
-        def turn(rows, word_block):
+        def turn(buf, word_block):
             grouped = grouped_tile()
+            words = buf[:].bitcast(F32).rearrange("p (j w) -> p j w", j=J)
+            dst = grouped[:].bitcast(F32).rearrange("q (j p u) -> q j p u", j=J, u=2)
             for half in range(2):
-                turn_half(rows, word_block, grouped, half)
+                bank = psum.tile([P, 2, 2, P], F32, name="turn_bank", tag="bank", bufs=BANK_BUFS)
+                for jj in range(2):
+                    for u in range(2):
+                        nc.tensor.transpose(bank[:, jj, u, :], word_block(words[:, 2 * half + jj, :], u), ident[:])
+                nc.scalar.copy(out=dst[:, 2 * half : 2 * half + 2], in_=bank[:].rearrange("q j u p -> q j p u"))
             return grouped
 
         def every_second(words, u):
             return words[:, u : W // 2 : 2]
 
-        def contiguous(words, u):
+        def side_by_side(words, u):
             return words[:, u * P : (u + 1) * P]
 
-        def interleave(engine, src, dst):
-            if engine == "gpsimd":
-                for a in range(4):
-                    n = src.shape[1] // 4
-                    s1 = src[:, a] if n == 1 else src[:, a * n : (a + 1) * n]
-                    d1 = dst[:, a] if n == 1 else dst[:, a * n : (a + 1) * n]
-                    nc.gpsimd.tensor_scalar(out=d1, in0=s1, scalar1=1.0, scalar2=0.0, op0=ALU.mult, op1=ALU.add)
-            elif engine == "both":
-                n = src.shape[1] // 2
-                nc.scalar.copy(out=dst[:, 0:n], in_=src[:, 0:n])
-                nc.vector.tensor_copy(out=dst[:, n : 2 * n], in_=src[:, n : 2 * n])
-            elif engine[0] == "s" and engine != "scalar":
-                n = int(engine[1:])
-                nc.scalar.copy(out=dst[:, 0:n], in_=src[:, 0:n])
-                nc.vector.tensor_copy(out=dst[:, n:], in_=src[:, n:])
-            else:
-                copy_on(engine, dst, src)
+        def copy_on_vector(dst, src):
+            nc.vector.tensor_copy(out=dst, in_=src)
+
+        def copy_on_scalar(dst, src):
+            nc.scalar.copy(out=dst, in_=src)
+
+        def copy_on_both(dst, src):
+            half = src.shape[1] // 2
+            copy_on_scalar(dst[:, 0:half], src[:, 0:half])
+            copy_on_vector(dst[:, half : 2 * half], src[:, half : 2 * half])
+
+        def copy_on_gpsimd(dst, src):
+            for j in range(J):
+                nc.gpsimd.tensor_scalar(out=dst[:, j], in0=src[:, j], scalar1=1.0, scalar2=0.0, op0=ALU.mult, op1=ALU.add)
+
 
         g_t, z_t, nf_t, edge_t, w_raw = {}, {}, {}, {}, {}
 
@@ -127,15 +124,15 @@ def tile_nodeupdatenetwork_pa_v_kernel(tc, node_feat, edge_feat, w0, denom, z, g
 
         def load_nf(t):
             nf_t[t] = load.tile([P, J * W], BF16, name="nf_rows", tag="nf_rows")
-            nc.sync.dma_start(out=slots(nf_t[t]), in_=node_feat[t].rearrange("(k p) d -> p k d", p=P))
+            nc.sync.dma_start(out=rows_of(nf_t[t]), in_=node_feat[t].rearrange("(j p) d -> p j d", p=P))
 
         def load_edge(s):
-            edge_t[s] = load.tile([P, J * W], BF16, name="edge_rows", tag="edge_rows", bufs=5)
+            edge_t[s] = load.tile([P, J * W], BF16, name="edge_rows", tag="edge_rows", bufs=EDGE_BUFS)
             load_nodes(edge_t[s], edge_feat[s // E, s % E])
 
         def load_w(c):
-            w_raw[c] = load.tile([P, J * W], BF16, name="w_rows", tag="w_rows", bufs=3)
-            nc.sync.dma_start(out=slots(w_raw[c]), in_=w0[:, c * W : (c + 1) * W].rearrange("(p j) c -> p j c", j=J))
+            w_raw[c] = load.tile([P, J * W], BF16, name="w_rows", tag="w_rows", bufs=E + 1)
+            nc.sync.dma_start(out=rows_of(w_raw[c]), in_=w0[:, c * W : (c + 1) * W].rearrange("(p j) c -> p j c", j=J))
 
         ctx.enter_context(tc.manual_schedule())
 
@@ -152,6 +149,8 @@ def tile_nodeupdatenetwork_pa_v_kernel(tc, node_feat, edge_feat, w0, denom, z, g
         load_nf(1)
         load_edge(2)
         load_edge(3)
+
+
         ident = const.tile([P, P], F32, name="ident")
         make_identity(nc, ident[:])
         den_sorted = const.tile([P, N], F32, name="den_sorted")
@@ -164,43 +163,44 @@ def tile_nodeupdatenetwork_pa_v_kernel(tc, node_feat, edge_feat, w0, denom, z, g
         nc.vector.memset(off_wide[:], 1.0)
         for j in range(2):
             nc.vector.tensor_copy(out=off_wide[:, j, :, j * J : (j + 1) * J], in_=off_runs[:, j])
-        rec = const.tile([P, J, T * E], F32, name="rec")
-        neg_rec = const.tile([P, J, T * E], F32, name="neg_rec")
+        rec = const.tile([P, J, STEPS], F32, name="rec")
+        neg_rec = const.tile([P, J, STEPS], F32, name="neg_rec")
 
         def turn_denominators():
             nc.vector.tensor_copy(
-                out=den_sorted[0 : T * E, :].rearrange("r (j k i) -> r j k i", j=J, i=J),
+                out=den_sorted[0:STEPS, :].rearrange("r (j k i) -> r j k i", j=J, i=J),
                 in_=den_rows[:].rearrange("r (k j i) -> r j k i", j=J, i=J),
             )
-            den_bank = psum.tile([P, J, P], F32, name="turn_bank", tag="bank", bufs=4)
+            bank = psum.tile([P, J, P], F32, name="turn_bank", tag="bank", bufs=BANK_BUFS)
             for j in range(J):
-                nc.tensor.transpose(den_bank[:, j, :], den_sorted[:, j * P : (j + 1) * P], ident[:])
-            return den_bank
+                nc.tensor.transpose(bank[:, j, :], den_sorted[:, j * P : (j + 1) * P], ident[:])
+            return bank
 
-        def reciprocals(den_bank):
-            nc.vector.reciprocal(out=rec[:], in_=den_bank[:, :, 0 : T * E])
+        def reciprocals(bank):
+            nc.vector.reciprocal(out=rec[:], in_=bank[:, :, 0:STEPS])
             nc.vector.tensor_scalar(out=neg_rec[:], in0=rec[:], scalar1=-1.0, scalar2=None, op0=ALU.mult)
 
-        w_g, w_q, dz2_t, dz2_g, dz2_q, nf_g, nf_q = {}, {}, {}, {}, {}, {}, {}
-        masked_g, masked_q, sign_t, dz1_t, dz1n_g, dz1n_q, dz1d_g, dz1d_q = {}, {}, {}, {}, {}, {}, {}, {}
-        result_t, neg_r_t, dm_t, moved_t = {}, {}, {}, {}
 
-        def group_w(c, engine):
+        w_g, w_q, dz2_t, dz2_g, dz2_q, nf_g, nf_q = {}, {}, {}, {}, {}, {}, {}
+        masked_g, masked_q, sign_t = {}, {}, {}
+        dx_t, dz1_t, dz1n_g, dz1n_q, dz1d_g, dz1d_q = {}, {}, {}, {}, {}, {}
+        dm_t, neg_r_t, dedge_t, node_bank, dnode_t = {}, {}, {}, {}, {}
+
+        def group_w(c):
             w_g[c] = grouped_tile()
-            interleave(
-                engine,
-                w_raw[c][:].rearrange("p (j q u e) -> p q j u e", j=J, u=2, e=2),
+            copy_on_vector(
                 w_g[c][:].rearrange("p (u q e j) -> p q j u e", u=2, e=2, j=J),
+                w_raw[c][:].rearrange("p (j q u e) -> p q j u e", j=J, u=2, e=2),
             )
 
         def quantize_w(c):
-            w_q[c] = quantize(w_g[c], E4, "w", 3)
+            w_q[c] = quantize(w_g[c], E4, "w", E + 1)
 
         def slope_factor(t, cols):
             nc.vector.tensor_scalar(out=z_t[t][:, cols], in0=z_t[t][:, cols], scalar1=0.0, scalar2=SLOPE, op0=ALU.is_ge, op1=ALU.max)
 
         def make_dz2(t, cols):
-            if t not in dz2_t:
+            if cols.start == 0:
                 dz2_t[t] = work.tile([P, J * W], BF16, name="dz2", tag="dz2")
             nc.vector.tensor_tensor(out=dz2_t[t][:, cols], in0=g_t[t][:, cols], in1=z_t[t][:, cols], op=ALU.mult)
 
@@ -217,76 +217,61 @@ def tile_nodeupdatenetwork_pa_v_kernel(tc, node_feat, edge_feat, w0, denom, z, g
             nf_q[t] = quantize(nf_g[t], E4, "nf", 2)
 
         def mask_edge(s):
-            runs = edge_t[s][:].rearrange("p (h j k y) -> p h j k y", h=2, j=2, y=16)
+            runs = edge_t[s][:].rearrange("p (h j k y) -> p h j k y", h=2, j=2, y=GROUP)
             for h in range(2):
-                part = runs[:, h, :, :, 8 * h : 8 * h + 8]
+                part = runs[:, h, :, :, 2 * J * h : 2 * J * (h + 1)]
                 nc.vector.tensor_tensor(out=part, in0=part, in1=off_wide[:], op=ALU.mult)
 
-        def group_edge(s, engine):
+        def group_edge(s, copy):
             masked_g[s] = grouped_tile()
-            interleave(
-                engine,
-                edge_t[s][:].rearrange("p (n k j i) -> p j k n i", n=J, j=J, i=J),
+            copy(
                 masked_g[s][:].rearrange("p (j k i n) -> p j k n i", n=J, j=J, i=J),
+                edge_t[s][:].rearrange("p (n k j i) -> p j k n i", n=J, j=J, i=J),
             )
 
         def quantize_edge(s):
-            masked_q[s] = quantize(masked_g[s], E4, "masked", 4)
+            masked_q[s] = quantize(masked_g[s], E4, "masked", 2 * E)
 
         def sign_edge(s):
             sign_t[s] = work.tile([P, J * W], BF16, name="sign", tag="sign", bufs=3)
             nc.scalar.activation(out=sign_t[s][:], in_=edge_t[s][:], func=ACT.Sign)
 
-        def sign_edge_split(s, n):
-            sign_t[s] = work.tile([P, J * W], BF16, name="sign", tag="sign", bufs=3)
-            if n > 0:
-                nc.scalar.activation(out=sign_t[s][:, 0:n], in_=edge_t[s][:, 0:n], func=ACT.Sign)
+        def make_dx(s):
+            for j in range(J):
+                dx_t[s, j] = psum.tile([P, W], F32, name="bank", tag="bank", bufs=BANK_BUFS)
+                mx_pass(dx_t[s, j], dz2_q[s // E], j, w_q[1 + s % E], True, True)
 
-        def sign_edge_rest(s, n):
-            if n < J * W:
-                nc.vector.tensor_scalar(out=sign_t[s][:, n:], in0=edge_t[s][:, n:], scalar1=2.0**34, scalar2=2.0**-100, op0=ALU.mult, op1=ALU.min)
-
-        def sign_edge_rest2(s, n):
-            if n < J * W:
-                nc.vector.tensor_scalar(out=sign_t[s][:, n:], in0=sign_t[s][:, n:], scalar1=-(2.0**-100), scalar2=2.0**100, op0=ALU.max, op1=ALU.mult)
-
-        dx_t, node_t = {}, {}
-
-        def make_dx(s, j):
-            dx_t[s, j] = psum.tile([P, W], F32, name="bank", tag="bank", bufs=4)
-            mx_pass(dx_t[s, j], dz2_q[s // E], j, w_q[1 + s % E], True, True)
-
-        def make_dz1(s, j):
-            if j == 0:
-                dz1_t[s] = work.tile([P, J * W], BF16, name="dz1", tag="dz1", bufs=2)
-            nc.scalar.activation(out=dz1_t[s][:, j * W : (j + 1) * W], in_=dx_t[s, j][:], func=ACT.Copy, scale=rec[:, j, s : s + 1])
+        def make_dz1(s):
+            dz1_t[s] = work.tile([P, J * W], BF16, name="dz1", tag="dz1")
+            for j in range(J):
+                nc.scalar.activation(out=dz1_t[s][:, j * W : (j + 1) * W], in_=dx_t[s, j][:], func=ACT.Copy, scale=rec[:, j, s : s + 1])
 
         def turn_dz1(s):
-            dz1d_g[s] = turn(dz1_t[s], contiguous)
+            dz1d_g[s] = turn(dz1_t[s], side_by_side)
 
         def quantize_dz1d(s):
             dz1d_q[s] = quantize(dz1d_g[s], E5, "dz1d", 2)
 
-        def group_dz1(s, engine):
+        def group_dz1(s, copy):
             dz1n_g[s] = grouped_tile()
-            interleave(
-                engine,
-                dz1_t[s][:].rearrange("p (j c i) -> p c j i", j=J, i=J),
+            copy(
                 dz1n_g[s][:].rearrange("p (c i j) -> p c j i", j=J, i=J),
+                dz1_t[s][:].rearrange("p (j c i) -> p c j i", j=J, i=J),
             )
 
         def quantize_dz1n(s):
-            dz1n_q[s] = quantize(dz1n_g[s], E5, "dz1n", 4)
+            dz1n_q[s] = quantize(dz1n_g[s], E5, "dz1n", 2 * E)
 
-        def make_dm(s, j):
-            dm_t[s, j] = psum.tile([P, W], F32, name="dm_bank", tag="dm_bank", bufs=4)
-            mx_pass(dm_t[s, j], dz1d_q[s], j, nf_q[s // E], True, True)
+        def make_dm(s):
+            for j in range(J):
+                dm_t[s, j] = psum.tile([P, W], F32, name="dm_bank", tag="dm_bank", bufs=BANK_BUFS)
+                mx_pass(dm_t[s, j], dz1d_q[s], j, nf_q[s // E], True, True)
 
         def row_sum(s, j):
             if j == 0:
-                result_t[s] = work.tile([P, PADDED], F32, name="edge_grad", tag="edge_grad", bufs=3)
+                dedge_t[s] = work.tile([P, PADDED], F32, name="edge_grad", tag="edge_grad", bufs=3)
                 neg_r_t[s] = work.tile([P, J], F32, name="neg_r", tag="neg_r", bufs=3)
-            products = work.tile([P, W], F32, name="products", tag="products", bufs=2)
+            products = work.tile([P, W], F32, name="products", tag="products")
             nc.vector.scalar_tensor_tensor(
                 out=products[:],
                 in0=dm_t[s, j][:],
@@ -297,9 +282,9 @@ def tile_nodeupdatenetwork_pa_v_kernel(tc, node_feat, edge_feat, w0, denom, z, g
                 accum_out=neg_r_t[s][:, j : j + 1],
             )
 
-        def finish(s, j):
+        def subtract_r(s, j):
             nc.vector.scalar_tensor_tensor(
-                out=result_t[s][:, j * W : (j + 1) * W],
+                out=dedge_t[s][:, j * W : (j + 1) * W],
                 in0=sign_t[s][:, j * W : (j + 1) * W],
                 scalar=neg_r_t[s][:, j : j + 1],
                 in1=dm_t[s, j][:],
@@ -307,125 +292,116 @@ def tile_nodeupdatenetwork_pa_v_kernel(tc, node_feat, edge_feat, w0, denom, z, g
                 op1=ALU.add,
             )
 
-        def store_edge_gradient(s, engine, js):
-            runs = diagonal_runs(result_t[s])[:, js]
+        def store_dedge(s, engine, js):
+            runs = diagonal_runs(dedge_t[s])[:, js]
             engine.tensor_tensor(out=runs, in0=runs, in1=off_runs[:, js], op=ALU.mult)
-            store_nodes(out_1[s // E, s % E], result_t[s], js)
+            store_nodes(out_1[s // E, s % E], dedge_t[s], js)
 
-        def node_gradient(t, js):
-            if js.start == 0:
-                node_t[t] = work.tile([P, J * W], F32, name="node_grad", tag="node_grad", bufs=2)
-            for j in range(js.start, js.stop):
-                bank = psum.tile([P, W], F32, name="bank", tag="bank", bufs=4)
-                mx_pass(bank, dz2_q[t], j, w_q[0], True, False)
-                mx_pass(bank, masked_q[E * t], j, dz1n_q[E * t], False, False)
-                mx_pass(bank, masked_q[E * t + 1], j, dz1n_q[E * t + 1], False, True)
-                nc.scalar.copy(
-                    out=node_t[t][:, j * W : (j + 1) * W].rearrange("p (q u e) -> p q u e", u=2, e=2),
-                    in_=bank[:].rearrange("p (u q e) -> p q u e", u=2, e=2),
-                )
+        def open_dnode(t, j):
+            node_bank[j] = psum.tile([P, W], F32, name="bank", tag="bank", bufs=BANK_BUFS)
+            mx_pass(node_bank[j], dz2_q[t], j, w_q[0], True, False)
+            mx_pass(node_bank[j], masked_q[E * t], j, dz1n_q[E * t], False, False)
 
-        def store_node_gradient(t, js):
-            store_nodes(out_0[t], node_t[t], js)
+        def close_dnode(t, j):
+            if j == 0:
+                dnode_t[t] = work.tile([P, J * W], F32, name="node_grad", tag="node_grad")
+            mx_pass(node_bank[j], masked_q[E * t + 1], j, dz1n_q[E * t + 1], False, True)
+            nc.scalar.copy(
+                out=dnode_t[t][:, j * W : (j + 1) * W].rearrange("p (q u e) -> p q u e", u=2, e=2),
+                in_=node_bank[j][:].rearrange("p (u q e) -> p q u e", u=2, e=2),
+            )
 
-        whole = slice(0, J * W)
-        halves = [slice(0, 2 * W), slice(2 * W, J * W)]
+        all_cols = slice(0, J * W)
+        col_halves = [slice(0, 2 * W), slice(2 * W, J * W)]
+        all_rows = slice(0, J)
+        row_halves = [slice(0, 2), slice(2, J)]
+
+        def read_dm_first(s):
+            row_sum(s, 0)
+            for j in range(1, J - 1):
+                row_sum(s, j)
+                subtract_r(s, j - 1)
+            row_sum(s, J - 1)
+
+        def read_dm_rest(s):
+            subtract_r(s, J - 2)
+            subtract_r(s, J - 1)
 
         den_bank = turn_denominators()
-        group_w(1, "vector")
+        group_w(1)
         mask_edge(0)
         sign_edge(0)
-        group_edge(0, "scalar")
+        group_edge(0, copy_on_scalar)
         reciprocals(den_bank)
         quantize_w(1)
-        for cols in halves:
+        for cols in col_halves:
             slope_factor(0, cols)
-        for cols in halves:
+        for cols in col_halves:
             make_dz2(0, cols)
         turn_dz2(0)
         turn_nf(0)
-        group_w(2, "vector")
+        group_w(2)
         quantize_edge(0)
         quantize_dz2(0)
-        for j in range(J):
-            make_dx(0, j)
+        make_dx(0)
         quantize_w(2)
-        group_w(0, "vector")
+        group_w(0)
         quantize_nf(0)
-        slope_factor(1, whole)
-        make_dz2(1, whole)
+        slope_factor(1, all_cols)
+        make_dz2(1, all_cols)
 
-        last = T * E
-        for s in range(last + 1):
+        make_dz1(0)
+        turn_dz1(0)
+        make_dx(1)
+        quantize_dz1d(0)
+        make_dm(0)
+        group_dz1(0, copy_on_scalar)
+        quantize_w(0)
+        mask_edge(1)
+        load_gz(2)
+        load_edge(EDGE_BUFS - 1)
+
+        for s in range(1, STEPS):
             t, e = divmod(s, E)
-            more = t + 1 < T
-            if 0 < s < last:
-                group_edge(s, "gpsimd")
-                if s > 1 and False:
-                    store_edge_gradient(s - 2, nc.gpsimd, slice(0, J))
-            if s < last:
+            next_graph = t + 1 < T
+            group_edge(s, copy_on_gpsimd)
+            if s >= 2:
+                store_dedge(s - 2, nc.gpsimd, all_rows)
+            make_dz1(s)
+            if e == 1 and next_graph:
+                turn_dz2(t + 1)
+            turn_dz1(s)
+            read_dm_first(s - 1)
+            read_dm_rest(s - 1)
+            if s == STEPS - 1:
                 for j in range(J):
-                    make_dz1(s, j)
-                if e == 1 and more:
-                    turn_dz2(t + 1)
-                turn_dz1(s)
-            if s > 0:
-                if s == last:
-                    node_gradient(t - 1, slice(0, 2))
-                    store_node_gradient(t - 1, slice(0, 2))
-                    node_gradient(t - 1, slice(2, J))
-                    store_node_gradient(t - 1, slice(2, J))
-                row_sum(s - 1, 0)
-                row_sum(s - 1, 1)
-                finish(s - 1, 0)
-                row_sum(s - 1, 2)
-                finish(s - 1, 1)
-                row_sum(s - 1, 3)
-                if s == last:
-                    store_edge_gradient(s - 1, nc.vector, slice(0, 2))
-                finish(s - 1, 2)
-                finish(s - 1, 3)
-            if s == last:
-                store_edge_gradient(s - 1, nc.vector, slice(2, J))
-                break
-            if s == 0:
-                for j in range(J):
-                    make_dx(s + 1, j)
+                    open_dnode(t, j)
                 quantize_dz1d(s)
-                for j in range(J):
-                    make_dm(s, j)
-                group_dz1(s, "scalar")
-                quantize_w(0)
-                mask_edge(1)
-                load_gz(2)
-            elif s == last - 1:
-                quantize_dz1d(s)
-                for j in range(J):
-                    make_dm(s, j)
-                group_dz1(s, "both")
+                store_dedge(s - 1, nc.vector, all_rows)
+                make_dm(s)
+                group_dz1(s, copy_on_both)
                 sign_edge(s)
-                store_edge_gradient(s - 1, nc.vector, slice(0, J))
-                quantize_dz1n(s - 1)
                 quantize_edge(s)
                 quantize_dz1n(s)
             elif e == 0:
                 quantize_dz1n(s - 1)
                 sign_edge(s)
                 quantize_dz1d(s)
-                if not False:
-                    store_edge_gradient(s - 1, nc.vector, slice(0, J))
-                node_gradient(t - 1, slice(0, J))
-                store_node_gradient(t - 1, slice(0, J))
                 for j in range(J):
-                    make_dm(s, j)
-                for j in range(J):
-                    make_dx(s + 1, j)
-                group_dz1(s, "both" if more else "vector")
-                if more:
-                    slope_factor(t + 1, whole)
-                quantize_edge(s)
-                if more:
-                    make_dz2(t + 1, whole)
+                    open_dnode(t - 1, j)
+                    close_dnode(t - 1, j)
+                store_nodes(out_0[t - 1], dnode_t[t - 1], all_rows)
+                make_dm(s)
+                make_dx(s + 1)
+                if next_graph:
+                    group_dz1(s, copy_on_both)
+                    slope_factor(t + 1, all_cols)
+                    quantize_edge(s)
+                    make_dz2(t + 1, all_cols)
+                else:
+                    group_dz1(s, copy_on_vector)
+                    quantize_edge(s)
+                    quantize_dz1n(s)
                 mask_edge(s + 1)
                 if t + 2 < T:
                     load_gz(t + 2)
@@ -435,19 +411,22 @@ def tile_nodeupdatenetwork_pa_v_kernel(tc, node_feat, edge_feat, w0, denom, z, g
                 sign_edge(s)
                 turn_nf(t + 1)
                 quantize_dz1d(s)
-                if not False:
-                    store_edge_gradient(s - 1, nc.vector, slice(0, J))
-                for j in range(J):
-                    make_dm(s, j)
-                for j in range(J):
-                    make_dx(s + 1, j)
-                group_dz1(s, "scalar")
+                make_dm(s)
+                make_dx(s + 1)
+                group_dz1(s, copy_on_scalar)
                 quantize_edge(s)
-                if s == 1 and False:
-                    quantize_w(0)
                 quantize_nf(t + 1)
                 mask_edge(s + 1)
                 if t + 2 < T:
                     load_nf(t + 2)
-            if s + 4 < last:
-                load_edge(s + 4)
+            if s + EDGE_BUFS - 1 < STEPS:
+                load_edge(s + EDGE_BUFS - 1)
+
+        for js in row_halves:
+            for j in range(js.start, js.stop):
+                close_dnode(T - 1, j)
+            store_nodes(out_0[T - 1], dnode_t[T - 1], js)
+        read_dm_first(STEPS - 1)
+        store_dedge(STEPS - 1, nc.vector, row_halves[0])
+        read_dm_rest(STEPS - 1)
+        store_dedge(STEPS - 1, nc.vector, row_halves[1])

from contextlib import ExitStack

import concourse.mybir as mybir
from concourse.masks import make_identity

T, N, D, E, H = 4, 512, 512, 2, 512
C = (E + 1) * D
SLOPE = 0.01
FLOPS = 2 * T * N * H * C + 2 * 2 * T * E * N * N * D

F32 = mybir.dt.float32
BF16 = mybir.dt.bfloat16
U32 = mybir.dt.uint32
U8 = mybir.dt.uint8
E4 = mybir.dt.float8_e4m3fn_x4
E5 = mybir.dt.float8_e5m2_x4
ALU = mybir.AluOpType
ACT = mybir.ActivationFunctionType

P = 128
J = 4
W = 512
GROUP = J * J
SKEW = W + J
PADDED = J * SKEW
STEPS = T * E

GROUPED_BUFS = 7
EDGE_BUFS = 5
BANK_BUFS = 4


def tile_nodeupdatenetwork_pa_v_kernel(tc, node_feat, edge_feat, w0, denom, z, grad_out, out_0, out_1):
    nc = tc.nc

    with ExitStack() as ctx:
        const = ctx.enter_context(tc.tile_pool(name="const", bufs=1))
        load = ctx.enter_context(tc.tile_pool(name="load", bufs=2))
        work = ctx.enter_context(tc.tile_pool(name="work", bufs=2))
        quant = ctx.enter_context(tc.tile_pool(name="quant", bufs=2))
        psum = ctx.enter_context(tc.psum_pool(name="psum", bufs=1))


        def node_rows(matrix, i):
            return matrix.rearrange("(k j i) w -> i k j w", j=J, i=J)[i]

        def rows_of(buf):
            return buf[:, 0 : J * W].rearrange("p (j w) -> p j w", j=J)

        def load_nodes(buf, matrix):
            for i in range(J):
                nc.sync.dma_start(out=rows_of(buf)[i:P:J], in_=node_rows(matrix, i))

        def store_nodes(matrix, buf, js):
            for i in range(J):
                nc.sync.dma_start(out=node_rows(matrix, i)[:, js], in_=rows_of(buf)[i:P:J, js])

        def diagonal_runs(buf):
            skewed = buf[:].rearrange("p (j x) -> p j x", x=SKEW)[:, :, 0:W]
            return skewed.rearrange("p j (k y) -> p j k y", y=GROUP)[:, :, :, 0:J]

        def grouped_tile():
            return work.tile([P, J * W], BF16, name="grouped", tag="grouped", bufs=GROUPED_BUFS, align_bytes=64)

        def quantize(grouped, fmt, tag, bufs):
            codes = quant.tile([P, W], U32, name=tag + "_codes", tag=tag + "_codes", bufs=bufs, align_bytes=64)
            scales = quant.tile([P, W], U8, name=tag + "_scales", tag=tag + "_scales", bufs=bufs, align_bytes=64)
            nc.vector.quantize_mx(out=codes[:].bitcast(fmt), scales=scales[:], in_=grouped[:])
            return codes, scales, fmt

        def mx_pass(acc, stationary, j, moving, start, stop):
            cols = slice(j * P, (j + 1) * P)
            nc.tensor.matmul_mx(
                out=acc[:],
                lhsT=stationary[0][:, cols].bitcast(stationary[2]),
                lhsT_scale=stationary[1][:, cols],
                rhs=moving[0][:].bitcast(moving[2]),
                rhs_scale=moving[1][:],
                start=start,
                stop=stop,
            )

        def turn(buf, word_block):
            grouped = grouped_tile()
            words = buf[:].bitcast(F32).rearrange("p (j w) -> p j w", j=J)
            dst = grouped[:].bitcast(F32).rearrange("q (j p u) -> q j p u", j=J, u=2)
            for half in range(2):
                bank = psum.tile([P, 2, 2, P], F32, name="turn_bank", tag="bank", bufs=BANK_BUFS)
                for jj in range(2):
                    for u in range(2):
                        nc.tensor.transpose(bank[:, jj, u, :], word_block(words[:, 2 * half + jj, :], u), ident[:])
                nc.scalar.copy(out=dst[:, 2 * half : 2 * half + 2], in_=bank[:].rearrange("q j u p -> q j p u"))
            return grouped

        def every_second(words, u):
            return words[:, u : W // 2 : 2]

        def side_by_side(words, u):
            return words[:, u * P : (u + 1) * P]

        def copy_on_vector(dst, src):
            nc.vector.tensor_copy(out=dst, in_=src)

        def copy_on_scalar(dst, src):
            nc.scalar.copy(out=dst, in_=src)

        def copy_on_both(dst, src):
            half = src.shape[1] // 2
            copy_on_scalar(dst[:, 0:half], src[:, 0:half])
            copy_on_vector(dst[:, half : 2 * half], src[:, half : 2 * half])

        def copy_on_gpsimd(dst, src):
            for j in range(J):
                nc.gpsimd.tensor_scalar(out=dst[:, j], in0=src[:, j], scalar1=1.0, scalar2=0.0, op0=ALU.mult, op1=ALU.add)


        g_t, z_t, nf_t, edge_t, w_raw = {}, {}, {}, {}, {}

        def load_gz(t):
            z_t[t] = load.tile([P, J * W], F32, name="z_rows", tag="z_rows")
            load_nodes(z_t[t], z[t])
            g_t[t] = load.tile([P, J * W], BF16, name="g_rows", tag="g_rows")
            load_nodes(g_t[t], grad_out[t])

        def load_nf(t):
            nf_t[t] = load.tile([P, J * W], BF16, name="nf_rows", tag="nf_rows")
            nc.sync.dma_start(out=rows_of(nf_t[t]), in_=node_feat[t].rearrange("(j p) d -> p j d", p=P))

        def load_edge(s):
            edge_t[s] = load.tile([P, J * W], BF16, name="edge_rows", tag="edge_rows", bufs=EDGE_BUFS)
            load_nodes(edge_t[s], edge_feat[s // E, s % E])

        def load_w(c):
            w_raw[c] = load.tile([P, J * W], BF16, name="w_rows", tag="w_rows", bufs=E + 1)
            nc.sync.dma_start(out=rows_of(w_raw[c]), in_=w0[:, c * W : (c + 1) * W].rearrange("(p j) c -> p j c", j=J))

        ctx.enter_context(tc.manual_schedule())

        den_rows = const.tile([T * E, N], F32, name="den_rows")
        nc.sync.dma_start(out=den_rows[:], in_=denom.rearrange("t e n -> (t e) n"))
        load_w(1)
        load_edge(0)
        load_gz(0)
        load_nf(0)
        load_w(2)
        load_w(0)
        load_edge(1)
        load_gz(1)
        load_nf(1)
        load_edge(2)
        load_edge(3)


        ident = const.tile([P, P], F32, name="ident")
        make_identity(nc, ident[:])
        den_sorted = const.tile([P, N], F32, name="den_sorted")
        nc.gpsimd.memset(den_sorted[:], 1.0)
        off = const.tile([P, J, P], BF16, name="off")
        for j in range(J):
            nc.scalar.activation(out=off[:, j, :], in_=ident[:], func=ACT.Sign, scale=-1.0, bias=1.0)
        off_runs = off[:].rearrange("p j (k i) -> p j k i", i=J)
        off_wide = const.tile([P, 2, P // J, 2 * J], BF16, name="off_wide")
        nc.vector.memset(off_wide[:], 1.0)
        for j in range(2):
            nc.vector.tensor_copy(out=off_wide[:, j, :, j * J : (j + 1) * J], in_=off_runs[:, j])
        rec = const.tile([P, J, STEPS], F32, name="rec")
        neg_rec = const.tile([P, J, STEPS], F32, name="neg_rec")

        def turn_denominators():
            nc.vector.tensor_copy(
                out=den_sorted[0:STEPS, :].rearrange("r (j k i) -> r j k i", j=J, i=J),
                in_=den_rows[:].rearrange("r (k j i) -> r j k i", j=J, i=J),
            )
            bank = psum.tile([P, J, P], F32, name="turn_bank", tag="bank", bufs=BANK_BUFS)
            for j in range(J):
                nc.tensor.transpose(bank[:, j, :], den_sorted[:, j * P : (j + 1) * P], ident[:])
            return bank

        def reciprocals(bank):
            nc.vector.reciprocal(out=rec[:], in_=bank[:, :, 0:STEPS])
            nc.vector.tensor_scalar(out=neg_rec[:], in0=rec[:], scalar1=-1.0, scalar2=None, op0=ALU.mult)


        w_g, w_q, dz2_t, dz2_g, dz2_q, nf_g, nf_q = {}, {}, {}, {}, {}, {}, {}
        masked_g, masked_q, sign_t = {}, {}, {}
        dx_t, dz1_t, dz1n_g, dz1n_q, dz1d_g, dz1d_q = {}, {}, {}, {}, {}, {}
        dm_t, neg_r_t, dedge_t, node_bank, dnode_t = {}, {}, {}, {}, {}

        def group_w(c):
            w_g[c] = grouped_tile()
            copy_on_vector(
                w_g[c][:].rearrange("p (u q e j) -> p q j u e", u=2, e=2, j=J),
                w_raw[c][:].rearrange("p (j q u e) -> p q j u e", j=J, u=2, e=2),
            )

        def quantize_w(c):
            w_q[c] = quantize(w_g[c], E4, "w", E + 1)

        def slope_factor(t, cols):
            nc.vector.tensor_scalar(out=z_t[t][:, cols], in0=z_t[t][:, cols], scalar1=0.0, scalar2=SLOPE, op0=ALU.is_ge, op1=ALU.max)

        def make_dz2(t, cols):
            if cols.start == 0:
                dz2_t[t] = work.tile([P, J * W], BF16, name="dz2", tag="dz2")
            nc.vector.tensor_tensor(out=dz2_t[t][:, cols], in0=g_t[t][:, cols], in1=z_t[t][:, cols], op=ALU.mult)

        def turn_dz2(t):
            dz2_g[t] = turn(dz2_t[t], every_second)

        def quantize_dz2(t):
            dz2_q[t] = quantize(dz2_g[t], E5, "dz2", 3)

        def turn_nf(t):
            nf_g[t] = turn(nf_t[t], every_second)

        def quantize_nf(t):
            nf_q[t] = quantize(nf_g[t], E4, "nf", 2)

        def mask_edge(s):
            runs = edge_t[s][:].rearrange("p (h j k y) -> p h j k y", h=2, j=2, y=GROUP)
            for h in range(2):
                part = runs[:, h, :, :, 2 * J * h : 2 * J * (h + 1)]
                nc.vector.tensor_tensor(out=part, in0=part, in1=off_wide[:], op=ALU.mult)

        def group_edge(s, copy):
            masked_g[s] = grouped_tile()
            copy(
                masked_g[s][:].rearrange("p (j k i n) -> p j k n i", n=J, j=J, i=J),
                edge_t[s][:].rearrange("p (n k j i) -> p j k n i", n=J, j=J, i=J),
            )

        def quantize_edge(s):
            masked_q[s] = quantize(masked_g[s], E4, "masked", 2 * E)

        def sign_edge(s):
            sign_t[s] = work.tile([P, J * W], BF16, name="sign", tag="sign", bufs=3)
            nc.scalar.activation(out=sign_t[s][:], in_=edge_t[s][:], func=ACT.Sign)

        def make_dx(s):
            for j in range(J):
                dx_t[s, j] = psum.tile([P, W], F32, name="bank", tag="bank", bufs=BANK_BUFS)
                mx_pass(dx_t[s, j], dz2_q[s // E], j, w_q[1 + s % E], True, True)

        def make_dz1(s):
            dz1_t[s] = work.tile([P, J * W], BF16, name="dz1", tag="dz1")
            for j in range(J):
                nc.scalar.activation(out=dz1_t[s][:, j * W : (j + 1) * W], in_=dx_t[s, j][:], func=ACT.Copy, scale=rec[:, j, s : s + 1])

        def turn_dz1(s):
            dz1d_g[s] = turn(dz1_t[s], side_by_side)

        def quantize_dz1d(s):
            dz1d_q[s] = quantize(dz1d_g[s], E5, "dz1d", 2)

        def group_dz1(s, copy):
            dz1n_g[s] = grouped_tile()
            copy(
                dz1n_g[s][:].rearrange("p (c i j) -> p c j i", j=J, i=J),
                dz1_t[s][:].rearrange("p (j c i) -> p c j i", j=J, i=J),
            )

        def quantize_dz1n(s):
            dz1n_q[s] = quantize(dz1n_g[s], E5, "dz1n", 2 * E)

        def make_dm(s):
            for j in range(J):
                dm_t[s, j] = psum.tile([P, W], F32, name="dm_bank", tag="dm_bank", bufs=BANK_BUFS)
                mx_pass(dm_t[s, j], dz1d_q[s], j, nf_q[s // E], True, True)

        def row_sum(s, j):
            if j == 0:
                dedge_t[s] = work.tile([P, PADDED], F32, name="edge_grad", tag="edge_grad", bufs=3)
                neg_r_t[s] = work.tile([P, J], F32, name="neg_r", tag="neg_r", bufs=3)
            products = work.tile([P, W], F32, name="products", tag="products")
            nc.vector.scalar_tensor_tensor(
                out=products[:],
                in0=dm_t[s, j][:],
                scalar=neg_rec[:, j, s : s + 1],
                in1=edge_t[s][:, j * W : (j + 1) * W],
                op0=ALU.mult,
                op1=ALU.mult,
                accum_out=neg_r_t[s][:, j : j + 1],
            )

        def subtract_r(s, j):
            nc.vector.scalar_tensor_tensor(
                out=dedge_t[s][:, j * W : (j + 1) * W],
                in0=sign_t[s][:, j * W : (j + 1) * W],
                scalar=neg_r_t[s][:, j : j + 1],
                in1=dm_t[s, j][:],
                op0=ALU.mult,
                op1=ALU.add,
            )

        def store_dedge(s, engine, js):
            runs = diagonal_runs(dedge_t[s])[:, js]
            engine.tensor_tensor(out=runs, in0=runs, in1=off_runs[:, js], op=ALU.mult)
            store_nodes(out_1[s // E, s % E], dedge_t[s], js)

        def open_dnode(t, j):
            node_bank[j] = psum.tile([P, W], F32, name="bank", tag="bank", bufs=BANK_BUFS)
            mx_pass(node_bank[j], dz2_q[t], j, w_q[0], True, False)
            mx_pass(node_bank[j], masked_q[E * t], j, dz1n_q[E * t], False, False)

        def close_dnode(t, j):
            if j == 0:
                dnode_t[t] = work.tile([P, J * W], F32, name="node_grad", tag="node_grad")
            mx_pass(node_bank[j], masked_q[E * t + 1], j, dz1n_q[E * t + 1], False, True)
            nc.scalar.copy(
                out=dnode_t[t][:, j * W : (j + 1) * W].rearrange("p (q u e) -> p q u e", u=2, e=2),
                in_=node_bank[j][:].rearrange("p (u q e) -> p q u e", u=2, e=2),
            )

        all_cols = slice(0, J * W)
        col_halves = [slice(0, 2 * W), slice(2 * W, J * W)]
        all_rows = slice(0, J)
        row_halves = [slice(0, 2), slice(2, J)]

        def read_dm_first(s):
            row_sum(s, 0)
            for j in range(1, J - 1):
                row_sum(s, j)
                subtract_r(s, j - 1)
            row_sum(s, J - 1)

        def read_dm_rest(s):
            subtract_r(s, J - 2)
            subtract_r(s, J - 1)

        den_bank = turn_denominators()
        group_w(1)
        mask_edge(0)
        sign_edge(0)
        group_edge(0, copy_on_scalar)
        reciprocals(den_bank)
        quantize_w(1)
        for cols in col_halves:
            slope_factor(0, cols)
        for cols in col_halves:
            make_dz2(0, cols)
        turn_dz2(0)
        turn_nf(0)
        group_w(2)
        quantize_edge(0)
        quantize_dz2(0)
        make_dx(0)
        quantize_w(2)
        group_w(0)
        quantize_nf(0)
        slope_factor(1, all_cols)
        make_dz2(1, all_cols)

        make_dz1(0)
        turn_dz1(0)
        make_dx(1)
        quantize_dz1d(0)
        make_dm(0)
        group_dz1(0, copy_on_scalar)
        quantize_w(0)
        mask_edge(1)
        load_gz(2)
        load_edge(EDGE_BUFS - 1)

        for s in range(1, STEPS):
            t, e = divmod(s, E)
            next_graph = t + 1 < T
            group_edge(s, copy_on_gpsimd)
            if s >= 2:
                store_dedge(s - 2, nc.gpsimd, all_rows)
            make_dz1(s)
            if e == 1 and next_graph:
                turn_dz2(t + 1)
            turn_dz1(s)
            read_dm_first(s - 1)
            read_dm_rest(s - 1)
            if s == STEPS - 1:
                for j in range(J):
                    open_dnode(t, j)
                quantize_dz1d(s)
                store_dedge(s - 1, nc.vector, all_rows)
                make_dm(s)
                group_dz1(s, copy_on_both)
                sign_edge(s)
                quantize_edge(s)
                quantize_dz1n(s)
            elif e == 0:
                quantize_dz1n(s - 1)
                sign_edge(s)
                quantize_dz1d(s)
                for j in range(J):
                    open_dnode(t - 1, j)
                    close_dnode(t - 1, j)
                store_nodes(out_0[t - 1], dnode_t[t - 1], all_rows)
                make_dm(s)
                make_dx(s + 1)
                if next_graph:
                    group_dz1(s, copy_on_both)
                    slope_factor(t + 1, all_cols)
                    quantize_edge(s)
                    make_dz2(t + 1, all_cols)
                else:
                    group_dz1(s, copy_on_vector)
                    quantize_edge(s)
                    quantize_dz1n(s)
                mask_edge(s + 1)
                if t + 2 < T:
                    load_gz(t + 2)
            else:
                quantize_dz2(t + 1)
                quantize_dz1n(s - 1)
                sign_edge(s)
                turn_nf(t + 1)
                quantize_dz1d(s)
                make_dm(s)
                make_dx(s + 1)
                group_dz1(s, copy_on_scalar)
                quantize_edge(s)
                quantize_nf(t + 1)
                mask_edge(s + 1)
                if t + 2 < T:
                    load_nf(t + 2)
            if s + EDGE_BUFS - 1 < STEPS:
                load_edge(s + EDGE_BUFS - 1)

        for js in row_halves:
            for j in range(js.start, js.stop):
                close_dnode(T - 1, j)
            store_nodes(out_0[T - 1], dnode_t[T - 1], js)
        read_dm_first(STEPS - 1)
        store_dedge(STEPS - 1, nc.vector, row_halves[0])
        read_dm_rest(STEPS - 1)
        store_dedge(STEPS - 1, nc.vector, row_halves[1])
